import numpy as np
import ml_dtypes


BF16 = ml_dtypes.bfloat16


def bf(x):
    return np.asarray(x, np.float32).astype(BF16)


def f64(x):
    return np.asarray(x).astype(np.float64)


E2M1 = np.array([0.0, 0.5, 1.0, 1.5, 2.0, 3.0, 4.0, 6.0, -0.0, -0.5, -1.0, -1.5, -2.0, -3.0, -4.0, -6.0])


def pack_weight(w, fmt):
    k, n = w.shape
    w = f64(bf(w)).reshape(k // 32, 32, n)
    amax = np.abs(w).max(1)
    if fmt == "e4m3":
        byte = np.frexp(amax)[1] - 1 + 127 - 7
    else:
        mant, ex = np.frexp(amax / 6.0)
        byte = np.where(mant > 0.5, ex, ex - 1) + 127
    byte = np.clip(np.where(amax > 0, byte, 1), 1, 254)
    scaled = (w * np.exp2(127.0 - byte)[:, None, :]).reshape(k, n).astype(np.float32)
    by_word = np.ascontiguousarray(scaled.reshape(k // 512, 128, 4, n).transpose(0, 1, 3, 2))
    if fmt == "e4m3":
        words = by_word.astype(ml_dtypes.float8_e4m3fn).view(np.uint8)
    else:
        c = by_word.astype(ml_dtypes.float4_e2m1fn).view(np.uint8) & 0xF
        words = c[..., 0::2] | (c[..., 1::2] << 4)
    return np.ascontiguousarray(words), np.ascontiguousarray(byte.astype(np.uint8).reshape(k // 512, 16, n))


def unpack_weight(words, scales, fmt):
    g, p, n, _ = words.shape
    if fmt == "e4m3":
        vals = np.ascontiguousarray(words).view(ml_dtypes.float8_e4m3fn).astype(np.float64)
    else:
        nib = np.empty((g, p, n, 4), np.uint8)
        nib[..., 0::2] = words & 0xF
        nib[..., 1::2] = words >> 4
        vals = E2M1[nib]
    vals = vals * np.repeat(np.exp2(scales.astype(np.float64) - 127.0), 8, axis=1)[..., None]
    return vals.transpose(0, 1, 3, 2).reshape(g * 512, n)

def pack4(w):
    words, scales = pack_weight(w, "e2m1")
    return words.reshape(words.shape[0], 128, -1), scales


def unpack4(words, scales):
    return unpack_weight(words.reshape(words.shape[0], 128, -1, 2), scales, "e2m1")


def kspread(k):
    return np.exp2(np.repeat(np.random.randint(-6, 7, k // 32), 32).astype(np.float64))


B, L, DIM, H, D = 2, 256, 2048, 16, 64
EPS = 1e-6
THETA = 10000.0


def rope_table(seq_len, head_dim):
    pos = np.arange(seq_len, dtype=np.float64)
    inv = 1.0 / (THETA ** (np.arange(0, head_dim, 2, dtype=np.float64) / head_dim))
    ang = pos[:, None] * inv[None, :]
    cos, sin = np.cos(ang), np.sin(ang)
    rot = np.stack([np.stack([cos, -sin], -1), np.stack([sin, cos], -1)], -2)
    return rot[None, None]


def rms_norm(u, gain):
    rrms = 1.0 / np.sqrt(np.mean(np.square(u), axis=-1, keepdims=True) + EPS)
    return u * rrms * gain


def rope(u, table):
    ur = u.reshape(*u.shape[:-1], -1, 1, 2)
    out = table[..., 0] * ur[..., 0] + table[..., 1] * ur[..., 1]
    return out.reshape(u.shape)


def setup_inputs():
    s = kspread(DIM)
    x = np.random.standard_normal((B, L, DIM)) * s
    x_words, x_scales = pack4(x.reshape(B * L, DIM).T)
    pe = bf(rope_table(L, D))
    words, scales = pack4(np.random.standard_normal((DIM, 3 * H * D)) / np.sqrt(DIM) / s[:, None])
    qkv_b = bf(np.random.standard_normal(3 * H * D) * 0.2)
    q_scale = bf(1.0 + 0.1 * np.random.standard_normal(D))
    k_scale = bf(1.0 + 0.1 * np.random.standard_normal(D))
    return {"x_words": x_words,
            "x_scales": x_scales,
            "pe": pe,
            "qkv_w_words": words,
            "qkv_w_scales": scales,
            "qkv_b": qkv_b,
            "q_scale": q_scale,
            "k_scale": k_scale}


def reference(x_words, x_scales, pe, qkv_w_words, qkv_w_scales, qkv_b, q_scale, k_scale):
    x = unpack4(x_words, x_scales).T.reshape(B, L, DIM)
    qkv = (x @ unpack4(qkv_w_words, qkv_w_scales)) + f64(qkv_b)
    qkv = qkv.reshape(B, L, 3, H, D).transpose(2, 0, 3, 1, 4)
    q, k, v = qkv[0], qkv[1], qkv[2]
    q = rms_norm(q, f64(q_scale))
    k = rms_norm(k, f64(k_scale))
    table = f64(pe)
    return rope(q, table), rope(k, table), v

@@ -1,0 +1,271 @@
+from contextlib import ExitStack
+
+import concourse.mybir as mybir
+from concourse.masks import make_identity
+
+F32 = mybir.dt.float32
+BF16 = mybir.dt.bfloat16
+I32 = mybir.dt.int32
+U8 = mybir.dt.uint8
+FP4X4 = mybir.dt.float4_e2m1fn_x4
+ALU = mybir.AluOpType
+ACT = mybir.ActivationFunctionType
+
+P = 128
+PASSES = 4
+NTOK = 512
+NB = 512
+HB = 8
+D = 64
+NBLK = 6
+QK_BLOCKS = 4
+EPS = 1e-6
+CODE_GROUPS = ((0, 1), (1, 2), (4, 6), (2, 4))
+BLOCK_ORDER = (0, 0, 0, 0, 1, 4, 1, 1, 4, 1, 4, 4, 2, 2, 2, 2, 5, 3, 5, 5, 3, 3, 3, 5)
+AHEAD = 7
+LAG = 3
+GPSIMD_T1 = (0, 9, 13)
+VECTOR_ADD = (22,)
+BROW = 384
+
+FLOPS = 2 * 512 * 2048 * 3072
+
+
+def tile_selfattention_pa_kernel(
+    tc, x_words, x_scales, pe, qkv_w_words, qkv_w_scales, qkv_b, q_scale, k_scale, out_0, out_1, out_2
+):
+    nc = tc.nc
+    outs = (out_0, out_1, out_2)
+
+    with ExitStack() as ctx:
+        keep = ctx.enter_context(tc.tile_pool(name="keep", bufs=1))
+        work = ctx.enter_context(tc.tile_pool(name="work", bufs=2))
+        ptab = ctx.enter_context(tc.psum_pool(name="ptab", bufs=1))
+        pacc = ctx.enter_context(tc.psum_pool(name="pacc", bufs=AHEAD))
+        ctx.enter_context(tc.manual_schedule())
+
+        brow = keep.tile([P, BROW], BF16, name="brow")
+        xs = keep.tile([P, PASSES, NTOK], U8, name="xs", align_bytes=64)
+        xc = keep.tile([P, PASSES, 2 * NTOK], U8, name="xc", align_bytes=64)
+        ws0 = keep.tile([P, PASSES, NB], U8, name="ws0", align_bytes=64)
+        ws1 = keep.tile([P, PASSES, (NBLK - 1) * NB], U8, name="ws1", align_bytes=64)
+        wc = []
+        for gi, (b0, b1) in enumerate(CODE_GROUPS):
+            wc_t = keep.tile([P, PASSES, 2 * (b1 - b0) * NB], U8, name="wc%d" % gi, align_bytes=64)
+            wc.append(wc_t)
+        pe_sb = keep.tile([P, 2, 2 * D], BF16, name="pe_sb")
+        gsb = keep.tile([P, 2, D], F32, name="gsb")
+        bias = keep.tile([P, NBLK * NB], BF16, name="bias")
+        one = keep.tile([P, 1], F32, name="one")
+        warm = keep.tile([P, 1], F32, name="warm")
+        ident = keep.tile([P, P], F32, name="ident")
+        identb = keep.tile([P, P], BF16, name="identb")
+        tabs = keep.tile([P, 2, 2, 2, D], F32, name="tabs")
+        tab_ps = ptab.tile([P, 2, 2, 2, D], F32, name="tab_ps")
+
+        nc.vector.memset(brow[:], 0.0)
+        nc.vector.memset(xs[:].bitcast(I32), 0)
+        nc.vector.memset(ws0[:].bitcast(I32), 0)
+        nc.gpsimd.memset(one[:], 1.0)
+        make_identity(nc, identb[:])
+        make_identity(nc, ident[:])
+        nc.gpsimd.memset(ws1[:].bitcast(F32), 0.0)
+        nc.scalar.activation(out=warm[:], in_=one[:], func=ACT.Abs_reciprocal_sqrt)
+
+        def load_scales(plane, src):
+            for q in range(4):
+                nc.sync.dma_start(
+                    out=plane[32 * q : 32 * q + 4, :, :].bitcast(I32),
+                    in_=src[:, 4 * q : 4 * q + 4, :].rearrange("g r n -> r g n").bitcast(I32),
+                )
+
+        nc.sync.dma_start(out=brow[8:9, 0:D], in_=q_scale.unsqueeze(0))
+        nc.sync.dma_start(out=brow[8:9, D : 2 * D], in_=k_scale.unsqueeze(0))
+        nc.sync.dma_start(out=brow[0:8, :], in_=qkv_b.rearrange("(r c) -> r c", c=BROW))
+        nc.sync.dma_start(out=pe_sb[:], in_=pe.rearrange("a b (t m) i r c -> (a b m) t (i r c)", t=2))
+        load_scales(xs, x_scales)
+        load_scales(ws0, qkv_w_scales[:, :, 0:NB])
+        nc.sync.dma_start(out=xc[:].bitcast(I32), in_=x_words.rearrange("g p n -> p g n").bitcast(I32))
+        for gi, (b0, b1) in enumerate(CODE_GROUPS):
+            nc.sync.dma_start(
+                out=wc[gi][:].bitcast(I32),
+                in_=qkv_w_words[:, :, 2 * b0 * NB : 2 * b1 * NB].rearrange("g p n -> p g n").bitcast(I32),
+            )
+            if gi == 0:
+                load_scales(ws1, qkv_w_scales[:, :, NB:])
+
+        def spread(r, width):
+            sp = pacc.tile([P, NB], F32, name="acc", tag="acc")
+            nc.tensor.matmul(
+                out=sp[:, 0:width], lhsT=identb[:, r : r + 1].to_broadcast([P, P]), rhs=brow[:, 0:width], start=True, stop=True
+            )
+            return sp
+
+        sp = spread(8, 2 * D)
+        nc.scalar.copy(out=gsb[:].rearrange("p s j -> p (s j)"), in_=sp[:, 0 : 2 * D])
+        for r in range(8):
+            sp = spread(r, BROW)
+            nc.scalar.copy(out=bias[:, BROW * r : BROW * (r + 1)], in_=sp[:, 0:BROW])
+
+        pe4 = pe_sb[:].rearrange("p t (i f) -> p t i f", f=4)
+        for s in range(2):
+            g2 = gsb[:, s, :].rearrange("p (i r) -> p i r", r=2)
+            nc.vector.tensor_tensor(
+                out=tabs[:, 0, s, :, :].rearrange("p t (i r) -> p t i r", r=2),
+                in0=pe4[:, :, :, 0:4:3],
+                in1=g2.unsqueeze(1).to_broadcast([P, 2, D // 2, 2]),
+                op=ALU.mult,
+            )
+            for r in range(2):
+                nc.vector.tensor_tensor(
+                    out=tabs[:, 1, s, :, :].rearrange("p t (i r) -> p t i r", r=2)[:, :, :, r],
+                    in0=pe4[:, :, :, 1 + r],
+                    in1=g2[:, :, 1 - r].unsqueeze(1).to_broadcast([P, 2, D // 2]),
+                    op=ALU.mult,
+                )
+        nc.tensor.matmul(
+            out=tab_ps[:].rearrange("p k s t j -> p (k s t j)"),
+            lhsT=ident[:],
+            rhs=tabs[:].rearrange("p k s t j -> p (k s t j)"),
+            start=True,
+            stop=True,
+        )
+
+        seen = {}
+        steps = []
+        for j in BLOCK_ORDER:
+            steps.append((j, seen.get(j, 0)))
+            seen[j] = seen.get(j, 0) + 1
+        nstep = len(steps)
+        acc = {}
+        ys = {}
+        t1s = {}
+        t2s = {}
+        rrs = {}
+        rss = {}
+        ress = {}
+
+        def group_of(j):
+            for gi, (b0, b1) in enumerate(CODE_GROUPS):
+                if b0 <= j < b1:
+                    return gi, j - b0
+            return None
+
+        def is_qk(i):
+            return 0 <= i < nstep and steps[i][0] < QK_BLOCKS
+
+        def mm(i):
+            j, u = steps[i]
+            gi, jj = group_of(j)
+            a = pacc.tile([P, NB], F32, name="acc", tag="acc")
+            for g in range(PASSES):
+                nc.tensor.matmul_mx(
+                    out=a[:],
+                    lhsT=xc[:, g, 2 * P * u : 2 * P * (u + 1)].bitcast(FP4X4),
+                    lhsT_scale=xs[:, g, P * u : P * (u + 1)],
+                    rhs=wc[gi][:, g, 2 * NB * jj : 2 * NB * (jj + 1)].bitcast(FP4X4),
+                    rhs_scale=(ws0[:, g, :] if j == 0 else ws1[:, g, NB * (j - 1) : NB * j]),
+                    start=(g == 0),
+                    stop=(g == PASSES - 1),
+                )
+            acc[i] = a
+
+        def bias_add(i):
+            j, u = steps[i]
+            if is_qk(i):
+                y = work.tile([P, NB], F32, name="y", tag="y", bufs=4)
+                ys[i] = y
+            else:
+                y = work.tile([P, NB], F32, name="res", tag="res", bufs=6)
+                ress[i] = y
+            nc.vector.tensor_tensor(out=y[:], in0=bias[:, NB * j : NB * (j + 1)], in1=acc[i][:], op=ALU.add)
+
+        def squares(i):
+            ss = work.tile([P, HB], F32, name="ss", tag="ss", bufs=4)
+            junk = work.tile([P, NB], F32, name="junk", tag="junk", bufs=2)
+            for h in range(HB):
+                nc.scalar.activation(
+                    out=junk[:, D * h : D * (h + 1)],
+                    in_=ys[i][:, D * h : D * (h + 1)],
+                    func=ACT.Square,
+                    accum_out=ss[:, h : h + 1],
+                )
+            rs = work.tile([P, HB], F32, name="rs", tag="rs", bufs=6)
+            nc.scalar.activation(out=rs[:], in_=ss[:], func=ACT.Abs_reciprocal_sqrt, scale=1.0 / D, bias=EPS)
+            rss[i] = rs
+
+        def rope(i):
+            j, u = steps[i]
+            s = j // 2
+            t = u % 2
+            t1 = work.tile([P, NB], F32, name="t1", tag="t1", bufs=3)
+            t2 = work.tile([P, NB], F32, name="t2", tag="t2", bufs=3)
+            if i in GPSIMD_T1:
+                nc.gpsimd.tensor_tensor(
+                    out=t1[:].rearrange("p (h d) -> p h d", d=D),
+                    in0=ys[i][:].rearrange("p (h d) -> p h d", d=D),
+                    in1=tabs[:, 0, s, t, :].unsqueeze(1).to_broadcast([P, HB, D]),
+                    op=ALU.mult,
+                )
+            else:
+                nc.vector.tensor_tensor(
+                    out=t1[:].rearrange("p (h d) -> p h d", d=D),
+                    in0=ys[i][:].rearrange("p (h d) -> p h d", d=D),
+                    in1=tab_ps[:, 0, s, t, :].unsqueeze(1).to_broadcast([P, HB, D]),
+                    op=ALU.mult,
+                )
+            nc.vector.tensor_tensor(
+                out=t2[:].rearrange("p (h i e) -> p h i e", h=HB, e=2),
+                in0=ys[i][:].rearrange("p (h i e) -> p h i e", h=HB, e=2)[:, :, :, ::-1],
+                in1=tab_ps[:, 1, s, t, :].rearrange("p (i e) -> p i e", e=2).unsqueeze(1).to_broadcast([P, HB, D // 2, 2]),
+                op=ALU.mult,
+            )
+            t1s[i] = t1
+            t2s[i] = t2
+
+        def add(i):
+            rr = work.tile([P, NB], F32, name="rr", tag="rr", bufs=4)
+            eng = nc.vector if i in VECTOR_ADD else nc.gpsimd
+            eng.tensor_tensor(out=rr[:], in0=t1s[i][:], in1=t2s[i][:], op=ALU.add)
+            rrs[i] = rr
+
+        def scale(i):
+            res = work.tile([P, NB], F32, name="res", tag="res", bufs=6)
+            for h in range(HB):
+                nc.scalar.activation(
+                    out=res[:, D * h : D * (h + 1)],
+                    in_=rrs[i][:, D * h : D * (h + 1)],
+                    func=ACT.Copy,
+                    scale=rss[i][:, h : h + 1],
+                )
+            ress[i] = res
+
+        def store(i):
+            j, u = steps[i]
+            h0 = HB * (j % 2)
+            l0 = P * (u % 2)
+            nc.sync.dma_start(
+                out=outs[j // 2][u // 2, h0 : h0 + HB, l0 : l0 + P, :].rearrange("h l d -> l h d"),
+                in_=ress[i][:].rearrange("p (h d) -> p h d", d=D),
+            )
+
+        for i in range(AHEAD):
+            mm(i)
+        for i in range(nstep + LAG):
+            if i < nstep:
+                bias_add(i)
+                if not is_qk(i):
+                    store(i)
+                if i + AHEAD < nstep:
+                    mm(i + AHEAD)
+                if is_qk(i):
+                    squares(i)
+            if is_qk(i - 2) and (i - 2) in VECTOR_ADD:
+                add(i - 2)
+            if is_qk(i - 1):
+                rope(i - 1)
+                if (i - 1) not in VECTOR_ADD:
+                    add(i - 1)
+            if is_qk(i - LAG):
+                scale(i - LAG)
+                store(i - LAG)

@@ -20,12 +20,10 @@ D = 64
 NBLK = 6
 QK_BLOCKS = 4
 EPS = 1e-6
-CODE_GROUPS = ((0, 1), (1, 2), (4, 6), (2, 4))
-BLOCK_ORDER = (0, 0, 0, 0, 1, 4, 1, 1, 4, 1, 4, 4, 2, 2, 2, 2, 5, 3, 5, 5, 3, 3, 3, 5)
+CODE_GROUPS = ((0, 1), (4, 5), (1, 2), (2, 4), (5, 6))
 AHEAD = 7
-LAG = 3
-GPSIMD_T1 = (0, 9, 13)
-VECTOR_ADD = (22,)
+UH = 2 * HB
+GH = 5
 BROW = 384
 
 FLOPS = 2 * 512 * 2048 * 3072
@@ -131,19 +129,23 @@ def tile_selfattention_pa_kernel(
             stop=True,
         )
 
-        seen = {}
-        steps = []
-        for j in BLOCK_ORDER:
-            steps.append((j, seen.get(j, 0)))
-            seen[j] = seen.get(j, 0) + 1
-        nstep = len(steps)
+        tiles = []
+        vts = [(j, u) for j in range(QK_BLOCKS, NBLK) for u in range(4)]
+        for n in range(2 * QK_BLOCKS):
+            tiles.append((n // 2, n % 2, n, 0))
+            tiles.append((n // 2, n % 2 + 2, n, 1))
+            if n >= 1:
+                tiles.append(vts[n - 1] + (-1, 0))
+        tiles.append(vts[-1] + (-1, 0))
+        ntile = len(tiles)
+        last_unit = 2 * QK_BLOCKS - 1
         acc = {}
         ys = {}
+        sss = {}
         t1s = {}
         t2s = {}
         rrs = {}
         rss = {}
-        ress = {}
 
         def group_of(j):
             for gi, (b0, b1) in enumerate(CODE_GROUPS):
@@ -151,11 +153,8 @@ def tile_selfattention_pa_kernel(
                     return gi, j - b0
             return None
 
-        def is_qk(i):
-            return 0 <= i < nstep and steps[i][0] < QK_BLOCKS
-
         def mm(i):
-            j, u = steps[i]
+            j, u, n, c = tiles[i]
             gi, jj = group_of(j)
             a = pacc.tile([P, NB], F32, name="acc", tag="acc")
             for g in range(PASSES):
@@ -170,102 +169,116 @@ def tile_selfattention_pa_kernel(
                 )
             acc[i] = a
 
-        def bias_add(i):
-            j, u = steps[i]
-            if is_qk(i):
-                y = work.tile([P, NB], F32, name="y", tag="y", bufs=4)
-                ys[i] = y
-            else:
-                y = work.tile([P, NB], F32, name="res", tag="res", bufs=6)
-                ress[i] = y
-            nc.vector.tensor_tensor(out=y[:], in0=bias[:, NB * j : NB * (j + 1)], in1=acc[i][:], op=ALU.add)
-
-        def squares(i):
-            ss = work.tile([P, HB], F32, name="ss", tag="ss", bufs=4)
-            junk = work.tile([P, NB], F32, name="junk", tag="junk", bufs=2)
-            for h in range(HB):
-                nc.scalar.activation(
-                    out=junk[:, D * h : D * (h + 1)],
-                    in_=ys[i][:, D * h : D * (h + 1)],
-                    func=ACT.Square,
-                    accum_out=ss[:, h : h + 1],
-                )
-            rs = work.tile([P, HB], F32, name="rs", tag="rs", bufs=6)
-            nc.scalar.activation(out=rs[:], in_=ss[:], func=ACT.Abs_reciprocal_sqrt, scale=1.0 / D, bias=EPS)
-            rss[i] = rs
-
-        def rope(i):
-            j, u = steps[i]
-            s = j // 2
-            t = u % 2
-            t1 = work.tile([P, NB], F32, name="t1", tag="t1", bufs=3)
-            t2 = work.tile([P, NB], F32, name="t2", tag="t2", bufs=3)
-            if i in GPSIMD_T1:
-                nc.gpsimd.tensor_tensor(
-                    out=t1[:].rearrange("p (h d) -> p h d", d=D),
-                    in0=ys[i][:].rearrange("p (h d) -> p h d", d=D),
-                    in1=tabs[:, 0, s, t, :].unsqueeze(1).to_broadcast([P, HB, D]),
-                    op=ALU.mult,
-                )
-            else:
-                nc.vector.tensor_tensor(
-                    out=t1[:].rearrange("p (h d) -> p h d", d=D),
-                    in0=ys[i][:].rearrange("p (h d) -> p h d", d=D),
-                    in1=tab_ps[:, 0, s, t, :].unsqueeze(1).to_broadcast([P, HB, D]),
-                    op=ALU.mult,
-                )
-            nc.vector.tensor_tensor(
-                out=t2[:].rearrange("p (h i e) -> p h i e", h=HB, e=2),
-                in0=ys[i][:].rearrange("p (h i e) -> p h i e", h=HB, e=2)[:, :, :, ::-1],
-                in1=tab_ps[:, 1, s, t, :].rearrange("p (i e) -> p i e", e=2).unsqueeze(1).to_broadcast([P, HB, D // 2, 2]),
-                op=ALU.mult,
-            )
-            t1s[i] = t1
-            t2s[i] = t2
-
-        def add(i):
-            rr = work.tile([P, NB], F32, name="rr", tag="rr", bufs=4)
-            eng = nc.vector if i in VECTOR_ADD else nc.gpsimd
-            eng.tensor_tensor(out=rr[:], in0=t1s[i][:], in1=t2s[i][:], op=ALU.add)
-            rrs[i] = rr
-
-        def scale(i):
-            res = work.tile([P, NB], F32, name="res", tag="res", bufs=6)
-            for h in range(HB):
-                nc.scalar.activation(
-                    out=res[:, D * h : D * (h + 1)],
-                    in_=rrs[i][:, D * h : D * (h + 1)],
-                    func=ACT.Copy,
-                    scale=rss[i][:, h : h + 1],
-                )
-            ress[i] = res
-
-        def store(i):
-            j, u = steps[i]
+        def store(j, u, src):
             h0 = HB * (j % 2)
             l0 = P * (u % 2)
             nc.sync.dma_start(
                 out=outs[j // 2][u // 2, h0 : h0 + HB, l0 : l0 + P, :].rearrange("h l d -> l h d"),
-                in_=ress[i][:].rearrange("p (h d) -> p h d", d=D),
+                in_=src.rearrange("p (h d) -> p h d", d=D),
             )
+
+        def bias_add(i):
+            j, u, n, c = tiles[i]
+            bj = bias[:, NB * j : NB * (j + 1)]
+            if n < 0:
+                res = work.tile([P, NB], F32, name="res", tag="res", bufs=6)
+                nc.vector.tensor_tensor(out=res[:], in0=bj, in1=acc[i][:], op=ALU.add)
+                store(j, u, res[:])
+                return
+            if c == 0:
+                y_t = work.tile([P, 2 * NB], F32, name="y", tag="y", bufs=3)
+                ys[n] = y_t
+            nc.vector.tensor_tensor(out=ys[n][:, NB * c : NB * (c + 1)], in0=bj, in1=acc[i][:], op=ALU.add)
+
+        def squares(i):
+            j, u, n, c = tiles[i]
+            if c == 0:
+                ss_t = work.tile([P, UH], F32, name="ss", tag="ss", bufs=2)
+                sss[n] = ss_t
+            junk = work.tile([P, NB], F32, name="junk", tag="junk", bufs=2)
+            for h in range(HB):
+                nc.scalar.activation(
+                    out=junk[:, D * h : D * (h + 1)],
+                    in_=ys[n][:, NB * c + D * h : NB * c + D * (h + 1)],
+                    func=ACT.Square,
+                    accum_out=sss[n][:, HB * c + h : HB * c + h + 1],
+                )
+            if c == 1:
+                rs = work.tile([P, UH], F32, name="rs", tag="rs", bufs=3)
+                nc.scalar.activation(out=rs[:], in_=sss[n][:], func=ACT.Abs_reciprocal_sqrt, scale=1.0 / D, bias=EPS)
+                rss[n] = rs
+
+        def gpsimd_heads(n):
+            if n == 0:
+                return UH
+            if n == last_unit:
+                return 0
+            return GH
+
+        def rope(n):
+            s = n // 4
+            t = n % 2
+            gh = gpsimd_heads(n)
+            t1 = work.tile([P, 2 * NB], F32, name="t1", tag="t1", bufs=2)
+            t2 = work.tile([P, 2 * NB], F32, name="t2", tag="t2", bufs=2)
+            y = ys[n]
+            if gh > 0:
+                nc.gpsimd.tensor_tensor(
+                    out=t1[:, 0 : D * gh].rearrange("p (h d) -> p h d", d=D),
+                    in0=y[:, 0 : D * gh].rearrange("p (h d) -> p h d", d=D),
+                    in1=tabs[:, 0, s, t, :].unsqueeze(1).to_broadcast([P, gh, D]),
+                    op=ALU.mult,
+                )
+            nc.vector.tensor_tensor(
+                out=t2[:].rearrange("p (h i e) -> p h i e", h=UH, e=2),
+                in0=y[:].rearrange("p (h i e) -> p h i e", h=UH, e=2)[:, :, :, ::-1],
+                in1=tab_ps[:, 1, s, t, :].rearrange("p (i e) -> p i e", e=2).unsqueeze(1).to_broadcast([P, UH, D // 2, 2]),
+                op=ALU.mult,
+            )
+            if gh < UH:
+                nc.vector.tensor_tensor(
+                    out=t1[:, D * gh :].rearrange("p (h d) -> p h d", d=D),
+                    in0=y[:, D * gh :].rearrange("p (h d) -> p h d", d=D),
+                    in1=tab_ps[:, 0, s, t, :].unsqueeze(1).to_broadcast([P, UH - gh, D]),
+                    op=ALU.mult,
+                )
+            t1s[n] = t1
+            t2s[n] = t2
+
+        def add(n):
+            rr = work.tile([P, 2 * NB], F32, name="rr", tag="rr", bufs=3)
+            if n == last_unit:
+                for c in range(2):
+                    cs = slice(NB * c, NB * (c + 1))
+                    nc.gpsimd.tensor_tensor(out=rr[:, cs], in0=t1s[n][:, cs], in1=t2s[n][:, cs], op=ALU.add)
+            else:
+                nc.gpsimd.tensor_tensor(out=rr[:], in0=t1s[n][:], in1=t2s[n][:], op=ALU.add)
+            rrs[n] = rr
+
+        def scale(n):
+            for c in range(2):
+                res = work.tile([P, NB], F32, name="res", tag="res", bufs=6)
+                for h in range(HB):
+                    nc.scalar.activation(
+                        out=res[:, D * h : D * (h + 1)],
+                        in_=rrs[n][:, NB * c + D * h : NB * c + D * (h + 1)],
+                        func=ACT.Copy,
+                        scale=rss[n][:, HB * c + h : HB * c + h + 1],
+                    )
+                store(n // 2, n % 2 + 2 * c, res[:])
 
         for i in range(AHEAD):
             mm(i)
-        for i in range(nstep + LAG):
-            if i < nstep:
-                bias_add(i)
-                if not is_qk(i):
-                    store(i)
-                if i + AHEAD < nstep:
-                    mm(i + AHEAD)
-                if is_qk(i):
-                    squares(i)
-            if is_qk(i - 2) and (i - 2) in VECTOR_ADD:
-                add(i - 2)
-            if is_qk(i - 1):
-                rope(i - 1)
-                if (i - 1) not in VECTOR_ADD:
-                    add(i - 1)
-            if is_qk(i - LAG):
-                scale(i - LAG)
-                store(i - LAG)
+        for i in range(ntile):
+            bias_add(i)
+            if i + AHEAD < ntile:
+                mm(i + AHEAD)
+            if tiles[i][2] >= 0:
+                squares(i)
+            if i >= 1 and tiles[i - 1][3] == 1:
+                n = tiles[i - 1][2]
+                rope(n)
+                add(n)
+                if n >= 1:
+                    scale(n - 1)
+        scale(last_unit)

@@ -45,10 +45,11 @@ def tile_selfattention_pa_kernel(
         brow = keep.tile([P, BROW], BF16, name="brow")
         xs = keep.tile([P, PASSES, NTOK], U8, name="xs", align_bytes=64)
         xc = keep.tile([P, PASSES, 2 * NTOK], U8, name="xc", align_bytes=64)
-        ws0 = keep.tile([P, PASSES, NB], U8, name="ws0", align_bytes=64)
-        ws1 = keep.tile([P, PASSES, (NBLK - 1) * NB], U8, name="ws1", align_bytes=64)
+        ws = []
         wc = []
         for gi, (b0, b1) in enumerate(CODE_GROUPS):
+            ws_t = keep.tile([P, PASSES, (b1 - b0) * NB], U8, name="ws%d" % gi, align_bytes=64)
+            ws.append(ws_t)
             wc_t = keep.tile([P, PASSES, 2 * (b1 - b0) * NB], U8, name="wc%d" % gi, align_bytes=64)
             wc.append(wc_t)
         pe_sb = keep.tile([P, 2, 2 * D], BF16, name="pe_sb")
@@ -63,18 +64,19 @@ def tile_selfattention_pa_kernel(
 
         nc.vector.memset(brow[:], 0.0)
         nc.vector.memset(xs[:].bitcast(I32), 0)
-        nc.vector.memset(ws0[:].bitcast(I32), 0)
+        nc.vector.memset(ws[0][:].bitcast(I32), 0)
         nc.gpsimd.memset(one[:], 1.0)
         make_identity(nc, identb[:])
         make_identity(nc, ident[:])
-        nc.gpsimd.memset(ws1[:].bitcast(F32), 0.0)
+        for gi in range(1, len(CODE_GROUPS)):
+            nc.gpsimd.memset(ws[gi][:].bitcast(F32), 0.0)
         nc.scalar.activation(out=warm[:], in_=one[:], func=ACT.Abs_reciprocal_sqrt)
 
         def load_scales(plane, src):
-            for q in range(4):
+            for r in range(4):
                 nc.sync.dma_start(
-                    out=plane[32 * q : 32 * q + 4, :, :].bitcast(I32),
-                    in_=src[:, 4 * q : 4 * q + 4, :].rearrange("g r n -> r g n").bitcast(I32),
+                    out=plane[r : P : 32, :, :].bitcast(I32),
+                    in_=src[:, r : 16 : 4, :].rearrange("g q n -> q g n").bitcast(I32),
                 )
 
         nc.sync.dma_start(out=brow[8:9, 0:D], in_=q_scale.unsqueeze(0))
@@ -82,15 +84,14 @@ def tile_selfattention_pa_kernel(
         nc.sync.dma_start(out=brow[0:8, :], in_=qkv_b.rearrange("(r c) -> r c", c=BROW))
         nc.sync.dma_start(out=pe_sb[:], in_=pe.rearrange("a b (t m) i r c -> (a b m) t (i r c)", t=2))
         load_scales(xs, x_scales)
-        load_scales(ws0, qkv_w_scales[:, :, 0:NB])
-        nc.sync.dma_start(out=xc[:].bitcast(I32), in_=x_words.rearrange("g p n -> p g n").bitcast(I32))
         for gi, (b0, b1) in enumerate(CODE_GROUPS):
+            load_scales(ws[gi], qkv_w_scales[:, :, b0 * NB : b1 * NB])
+            if gi == 0:
+                nc.sync.dma_start(out=xc[:].bitcast(I32), in_=x_words.rearrange("g p n -> p g n").bitcast(I32))
             nc.sync.dma_start(
                 out=wc[gi][:].bitcast(I32),
                 in_=qkv_w_words[:, :, 2 * b0 * NB : 2 * b1 * NB].rearrange("g p n -> p g n").bitcast(I32),
             )
-            if gi == 0:
-                load_scales(ws1, qkv_w_scales[:, :, NB:])
 
         def spread(r, width):
             sp = pacc.tile([P, NB], F32, name="acc", tag="acc")
@@ -163,7 +164,7 @@ def tile_selfattention_pa_kernel(
                     lhsT=xc[:, g, 2 * P * u : 2 * P * (u + 1)].bitcast(FP4X4),
                     lhsT_scale=xs[:, g, P * u : P * (u + 1)],
                     rhs=wc[gi][:, g, 2 * NB * jj : 2 * NB * (jj + 1)].bitcast(FP4X4),
-                    rhs_scale=(ws0[:, g, :] if j == 0 else ws1[:, g, NB * (j - 1) : NB * j]),
+                    rhs_scale=ws[gi][:, g, NB * jj : NB * (jj + 1)],
                     start=(g == 0),
                     stop=(g == PASSES - 1),
                 )

@@ -72,8 +72,8 @@ def tile_selfattention_pa_kernel(
             nc.gpsimd.memset(ws[gi][:].bitcast(F32), 0.0)
         nc.scalar.activation(out=warm[:], in_=one[:], func=ACT.Abs_reciprocal_sqrt)
 
-        def load_scales(plane, src):
-            for r in range(4):
+        def load_scales(plane, src, r0=0, r1=4):
+            for r in range(r0, r1):
                 nc.sync.dma_start(
                     out=plane[r : P : 32, :, :].bitcast(I32),
                     in_=src[:, r : 16 : 4, :].rearrange("g q n -> q g n").bitcast(I32),
@@ -83,15 +83,22 @@ def tile_selfattention_pa_kernel(
         nc.sync.dma_start(out=brow[8:9, D : 2 * D], in_=k_scale.unsqueeze(0))
         nc.sync.dma_start(out=brow[0:8, :], in_=qkv_b.rearrange("(r c) -> r c", c=BROW))
         nc.sync.dma_start(out=pe_sb[:], in_=pe.rearrange("a b (t m) i r c -> (a b m) t (i r c)", t=2))
-        load_scales(xs, x_scales)
-        for gi, (b0, b1) in enumerate(CODE_GROUPS):
-            load_scales(ws[gi], qkv_w_scales[:, :, b0 * NB : b1 * NB])
-            if gi == 0:
-                nc.sync.dma_start(out=xc[:].bitcast(I32), in_=x_words.rearrange("g p n -> p g n").bitcast(I32))
+        def load_codes(gi):
+            b0, b1 = CODE_GROUPS[gi]
             nc.sync.dma_start(
                 out=wc[gi][:].bitcast(I32),
                 in_=qkv_w_words[:, :, 2 * b0 * NB : 2 * b1 * NB].rearrange("g p n -> p g n").bitcast(I32),
             )
+
+        load_scales(xs, x_scales, 0, 2)
+        nc.sync.dma_start(out=xc[:].bitcast(I32), in_=x_words.rearrange("g p n -> p g n").bitcast(I32))
+        load_codes(0)
+        load_scales(xs, x_scales, 2, 4)
+        load_scales(ws[0], qkv_w_scales[:, :, 0:NB])
+        for gi in range(1, len(CODE_GROUPS)):
+            b0, b1 = CODE_GROUPS[gi]
+            load_scales(ws[gi], qkv_w_scales[:, :, b0 * NB : b1 * NB])
+            load_codes(gi)
 
         def spread(r, width):
             sp = pacc.tile([P, NB], F32, name="acc", tag="acc")
@@ -135,9 +142,7 @@ def tile_selfattention_pa_kernel(
         for n in range(2 * QK_BLOCKS):
             tiles.append((n // 2, n % 2, n, 0))
             tiles.append((n // 2, n % 2 + 2, n, 1))
-            if n >= 1:
-                tiles.append(vts[n - 1] + (-1, 0))
-        tiles.append(vts[-1] + (-1, 0))
+            tiles.append(vts[n] + (-1, 0))
         ntile = len(tiles)
         last_unit = 2 * QK_BLOCKS - 1
         acc = {}
@@ -216,45 +221,46 @@ def tile_selfattention_pa_kernel(
                 return 0
             return GH
 
-        def rope(n):
+        def rope(n, lo, hi):
             s = n // 4
             t = n % 2
             gh = gpsimd_heads(n)
-            t1 = work.tile([P, 2 * NB], F32, name="t1", tag="t1", bufs=2)
-            t2 = work.tile([P, 2 * NB], F32, name="t2", tag="t2", bufs=2)
+            nh = (hi - lo) // D
+            if lo == 0:
+                t1_t = work.tile([P, 2 * NB], F32, name="t1", tag="t1", bufs=2)
+                t2_t = work.tile([P, 2 * NB], F32, name="t2", tag="t2", bufs=2)
+                t1s[n] = t1_t
+                t2s[n] = t2_t
+            t1 = t1s[n]
+            t2 = t2s[n]
             y = ys[n]
+            mid = lo + D * gh
             if gh > 0:
                 nc.gpsimd.tensor_tensor(
-                    out=t1[:, 0 : D * gh].rearrange("p (h d) -> p h d", d=D),
-                    in0=y[:, 0 : D * gh].rearrange("p (h d) -> p h d", d=D),
+                    out=t1[:, lo:mid].rearrange("p (h d) -> p h d", d=D),
+                    in0=y[:, lo:mid].rearrange("p (h d) -> p h d", d=D),
                     in1=tabs[:, 0, s, t, :].unsqueeze(1).to_broadcast([P, gh, D]),
                     op=ALU.mult,
                 )
             nc.vector.tensor_tensor(
-                out=t2[:].rearrange("p (h i e) -> p h i e", h=UH, e=2),
-                in0=y[:].rearrange("p (h i e) -> p h i e", h=UH, e=2)[:, :, :, ::-1],
-                in1=tab_ps[:, 1, s, t, :].rearrange("p (i e) -> p i e", e=2).unsqueeze(1).to_broadcast([P, UH, D // 2, 2]),
+                out=t2[:, lo:hi].rearrange("p (h i e) -> p h i e", h=nh, e=2),
+                in0=y[:, lo:hi].rearrange("p (h i e) -> p h i e", h=nh, e=2)[:, :, :, ::-1],
+                in1=tab_ps[:, 1, s, t, :].rearrange("p (i e) -> p i e", e=2).unsqueeze(1).to_broadcast([P, nh, D // 2, 2]),
                 op=ALU.mult,
             )
-            if gh < UH:
+            if gh < nh:
                 nc.vector.tensor_tensor(
-                    out=t1[:, D * gh :].rearrange("p (h d) -> p h d", d=D),
-                    in0=y[:, D * gh :].rearrange("p (h d) -> p h d", d=D),
-                    in1=tab_ps[:, 0, s, t, :].unsqueeze(1).to_broadcast([P, UH - gh, D]),
+                    out=t1[:, mid:hi].rearrange("p (h d) -> p h d", d=D),
+                    in0=y[:, mid:hi].rearrange("p (h d) -> p h d", d=D),
+                    in1=tab_ps[:, 0, s, t, :].unsqueeze(1).to_broadcast([P, nh - gh, D]),
                     op=ALU.mult,
                 )
-            t1s[n] = t1
-            t2s[n] = t2
 
-        def add(n):
-            rr = work.tile([P, 2 * NB], F32, name="rr", tag="rr", bufs=3)
-            if n == last_unit:
-                for c in range(2):
-                    cs = slice(NB * c, NB * (c + 1))
-                    nc.gpsimd.tensor_tensor(out=rr[:, cs], in0=t1s[n][:, cs], in1=t2s[n][:, cs], op=ALU.add)
-            else:
-                nc.gpsimd.tensor_tensor(out=rr[:], in0=t1s[n][:], in1=t2s[n][:], op=ALU.add)
-            rrs[n] = rr
+        def add(n, lo, hi):
+            if lo == 0:
+                rr_t = work.tile([P, 2 * NB], F32, name="rr", tag="rr", bufs=3)
+                rrs[n] = rr_t
+            nc.gpsimd.tensor_tensor(out=rrs[n][:, lo:hi], in0=t1s[n][:, lo:hi], in1=t2s[n][:, lo:hi], op=ALU.add)
 
         def scale(n):
             for c in range(2):
@@ -276,10 +282,16 @@ def tile_selfattention_pa_kernel(
                 mm(i + AHEAD)
             if tiles[i][2] >= 0:
                 squares(i)
-            if i >= 1 and tiles[i - 1][3] == 1:
-                n = tiles[i - 1][2]
-                rope(n)
-                add(n)
-                if n >= 1:
-                    scale(n - 1)
+            if i >= 1 and tiles[i - 1][2] >= 0:
+                n, c = tiles[i - 1][2:4]
+                if n == last_unit:
+                    rope(n, NB * c, NB * (c + 1))
+                    add(n, NB * c, NB * (c + 1))
+                    if c == 1:
+                        scale(n - 1)
+                elif c == 1:
+                    rope(n, 0, 2 * NB)
+                    add(n, 0, 2 * NB)
+                    if n >= 1:
+                        scale(n - 1)
         scale(last_unit)

@@ -24,6 +24,14 @@ CODE_GROUPS = ((0, 1), (4, 5), (1, 2), (2, 4), (5, 6))
 AHEAD = 7
 UH = 2 * HB
 GH = 5
+OFF_Y = 64
+OFF_JUNK = OFF_Y + 3 * 4096 + 128
+OFF_T1 = OFF_JUNK + 2 * 2048 + 192
+OFF_T2 = OFF_T1 + 2 * 4096
+OFF_RR = OFF_T2 + 2 * 4096 + 64
+OFF_RES = OFF_RR + 3 * 4096 + 64
+OFF_SS = OFF_RES + 6 * 2048
+OFF_RS = OFF_SS + 2 * 64
 BROW = 384
 
 FLOPS = 2 * 512 * 2048 * 3072
@@ -187,21 +195,21 @@ def tile_selfattention_pa_kernel(
             j, u, n, c = tiles[i]
             bj = bias[:, NB * j : NB * (j + 1)]
             if n < 0:
-                res = work.tile([P, NB], F32, name="res", tag="res", bufs=6)
+                res = work.tile([P, NB], F32, name="res", tag="res", bufs=6, offset=OFF_RES, align_bytes=256)
                 nc.vector.tensor_tensor(out=res[:], in0=bj, in1=acc[i][:], op=ALU.add)
                 store(j, u, res[:])
                 return
             if c == 0:
-                y_t = work.tile([P, 2 * NB], F32, name="y", tag="y", bufs=3)
+                y_t = work.tile([P, 2 * NB], F32, name="y", tag="y", bufs=3, offset=OFF_Y)
                 ys[n] = y_t
             nc.vector.tensor_tensor(out=ys[n][:, NB * c : NB * (c + 1)], in0=bj, in1=acc[i][:], op=ALU.add)
 
         def squares(i):
             j, u, n, c = tiles[i]
             if c == 0:
-                ss_t = work.tile([P, UH], F32, name="ss", tag="ss", bufs=2)
+                ss_t = work.tile([P, UH], F32, name="ss", tag="ss", bufs=2, offset=OFF_SS)
                 sss[n] = ss_t
-            junk = work.tile([P, NB], F32, name="junk", tag="junk", bufs=2)
+            junk = work.tile([P, NB], F32, name="junk", tag="junk", bufs=2, offset=OFF_JUNK)
             for h in range(HB):
                 nc.scalar.activation(
                     out=junk[:, D * h : D * (h + 1)],
@@ -210,7 +218,7 @@ def tile_selfattention_pa_kernel(
                     accum_out=sss[n][:, HB * c + h : HB * c + h + 1],
                 )
             if c == 1:
-                rs = work.tile([P, UH], F32, name="rs", tag="rs", bufs=3)
+                rs = work.tile([P, UH], F32, name="rs", tag="rs", bufs=3, offset=OFF_RS)
                 nc.scalar.activation(out=rs[:], in_=sss[n][:], func=ACT.Abs_reciprocal_sqrt, scale=1.0 / D, bias=EPS)
                 rss[n] = rs
 
@@ -227,8 +235,8 @@ def tile_selfattention_pa_kernel(
             gh = gpsimd_heads(n)
             nh = (hi - lo) // D
             if lo == 0:
-                t1_t = work.tile([P, 2 * NB], F32, name="t1", tag="t1", bufs=2)
-                t2_t = work.tile([P, 2 * NB], F32, name="t2", tag="t2", bufs=2)
+                t1_t = work.tile([P, 2 * NB], F32, name="t1", tag="t1", bufs=2, offset=OFF_T1)
+                t2_t = work.tile([P, 2 * NB], F32, name="t2", tag="t2", bufs=2, offset=OFF_T2)
                 t1s[n] = t1_t
                 t2s[n] = t2_t
             t1 = t1s[n]
@@ -258,13 +266,13 @@ def tile_selfattention_pa_kernel(
 
         def add(n, lo, hi):
             if lo == 0:
-                rr_t = work.tile([P, 2 * NB], F32, name="rr", tag="rr", bufs=3)
+                rr_t = work.tile([P, 2 * NB], F32, name="rr", tag="rr", bufs=3, offset=OFF_RR)
                 rrs[n] = rr_t
             nc.gpsimd.tensor_tensor(out=rrs[n][:, lo:hi], in0=t1s[n][:, lo:hi], in1=t2s[n][:, lo:hi], op=ALU.add)
 
         def scale(n):
             for c in range(2):
-                res = work.tile([P, NB], F32, name="res", tag="res", bufs=6)
+                res = work.tile([P, NB], F32, name="res", tag="res", bufs=6, offset=OFF_RES, align_bytes=256)
                 for h in range(HB):
                     nc.scalar.activation(
                         out=res[:, D * h : D * (h + 1)],

@@ -27,8 +27,8 @@ GH = 5
 OFF_Y = 64
 OFF_JUNK = OFF_Y + 3 * 4096 + 128
 OFF_T1 = OFF_JUNK + 2 * 2048 + 192
-OFF_T2 = OFF_T1 + 2 * 4096
-OFF_RR = OFF_T2 + 2 * 4096 + 64
+OFF_T2 = OFF_T1 + 2 * 4096 + 128
+OFF_RR = OFF_T2 + 2 * 4096 + 192
 OFF_RES = OFF_RR + 3 * 4096 + 64
 OFF_SS = OFF_RES + 6 * 2048
 OFF_RS = OFF_SS + 2 * 64

from contextlib import ExitStack

import concourse.mybir as mybir
from concourse.masks import make_identity

F32 = mybir.dt.float32
BF16 = mybir.dt.bfloat16
I32 = mybir.dt.int32
U8 = mybir.dt.uint8
FP4X4 = mybir.dt.float4_e2m1fn_x4
ALU = mybir.AluOpType
ACT = mybir.ActivationFunctionType

P = 128
PASSES = 4
NTOK = 512
NB = 512
HB = 8
D = 64
NBLK = 6
QK_BLOCKS = 4
EPS = 1e-6
CODE_GROUPS = ((0, 1), (4, 5), (1, 2), (2, 4), (5, 6))
AHEAD = 7
UH = 2 * HB
GH = 5
OFF_Y = 64
OFF_JUNK = OFF_Y + 3 * 4096 + 128
OFF_T1 = OFF_JUNK + 2 * 2048 + 192
OFF_T2 = OFF_T1 + 2 * 4096 + 128
OFF_RR = OFF_T2 + 2 * 4096 + 192
OFF_RES = OFF_RR + 3 * 4096 + 64
OFF_SS = OFF_RES + 6 * 2048
OFF_RS = OFF_SS + 2 * 64
BROW = 384

FLOPS = 2 * 512 * 2048 * 3072


def tile_selfattention_pa_kernel(
    tc, x_words, x_scales, pe, qkv_w_words, qkv_w_scales, qkv_b, q_scale, k_scale, out_0, out_1, out_2
):
    nc = tc.nc
    outs = (out_0, out_1, out_2)

    with ExitStack() as ctx:
        keep = ctx.enter_context(tc.tile_pool(name="keep", bufs=1))
        work = ctx.enter_context(tc.tile_pool(name="work", bufs=2))
        ptab = ctx.enter_context(tc.psum_pool(name="ptab", bufs=1))
        pacc = ctx.enter_context(tc.psum_pool(name="pacc", bufs=AHEAD))
        ctx.enter_context(tc.manual_schedule())

        brow = keep.tile([P, BROW], BF16, name="brow")
        xs = keep.tile([P, PASSES, NTOK], U8, name="xs", align_bytes=64)
        xc = keep.tile([P, PASSES, 2 * NTOK], U8, name="xc", align_bytes=64)
        ws = []
        wc = []
        for gi, (b0, b1) in enumerate(CODE_GROUPS):
            ws_t = keep.tile([P, PASSES, (b1 - b0) * NB], U8, name="ws%d" % gi, align_bytes=64)
            ws.append(ws_t)
            wc_t = keep.tile([P, PASSES, 2 * (b1 - b0) * NB], U8, name="wc%d" % gi, align_bytes=64)
            wc.append(wc_t)
        pe_sb = keep.tile([P, 2, 2 * D], BF16, name="pe_sb")
        gsb = keep.tile([P, 2, D], F32, name="gsb")
        bias = keep.tile([P, NBLK * NB], BF16, name="bias")
        one = keep.tile([P, 1], F32, name="one")
        warm = keep.tile([P, 1], F32, name="warm")
        ident = keep.tile([P, P], F32, name="ident")
        identb = keep.tile([P, P], BF16, name="identb")
        tabs = keep.tile([P, 2, 2, 2, D], F32, name="tabs")
        tab_ps = ptab.tile([P, 2, 2, 2, D], F32, name="tab_ps")

        nc.vector.memset(brow[:], 0.0)
        nc.vector.memset(xs[:].bitcast(I32), 0)
        nc.vector.memset(ws[0][:].bitcast(I32), 0)
        nc.gpsimd.memset(one[:], 1.0)
        make_identity(nc, identb[:])
        make_identity(nc, ident[:])
        for gi in range(1, len(CODE_GROUPS)):
            nc.gpsimd.memset(ws[gi][:].bitcast(F32), 0.0)
        nc.scalar.activation(out=warm[:], in_=one[:], func=ACT.Abs_reciprocal_sqrt)

        def load_scales(plane, src, r0=0, r1=4):
            for r in range(r0, r1):
                nc.sync.dma_start(
                    out=plane[r : P : 32, :, :].bitcast(I32),
                    in_=src[:, r : 16 : 4, :].rearrange("g q n -> q g n").bitcast(I32),
                )

        nc.sync.dma_start(out=brow[8:9, 0:D], in_=q_scale.unsqueeze(0))
        nc.sync.dma_start(out=brow[8:9, D : 2 * D], in_=k_scale.unsqueeze(0))
        nc.sync.dma_start(out=brow[0:8, :], in_=qkv_b.rearrange("(r c) -> r c", c=BROW))
        nc.sync.dma_start(out=pe_sb[:], in_=pe.rearrange("a b (t m) i r c -> (a b m) t (i r c)", t=2))
        def load_codes(gi):
            b0, b1 = CODE_GROUPS[gi]
            nc.sync.dma_start(
                out=wc[gi][:].bitcast(I32),
                in_=qkv_w_words[:, :, 2 * b0 * NB : 2 * b1 * NB].rearrange("g p n -> p g n").bitcast(I32),
            )

        load_scales(xs, x_scales, 0, 2)
        nc.sync.dma_start(out=xc[:].bitcast(I32), in_=x_words.rearrange("g p n -> p g n").bitcast(I32))
        load_codes(0)
        load_scales(xs, x_scales, 2, 4)
        load_scales(ws[0], qkv_w_scales[:, :, 0:NB])
        for gi in range(1, len(CODE_GROUPS)):
            b0, b1 = CODE_GROUPS[gi]
            load_scales(ws[gi], qkv_w_scales[:, :, b0 * NB : b1 * NB])
            load_codes(gi)

        def spread(r, width):
            sp = pacc.tile([P, NB], F32, name="acc", tag="acc")
            nc.tensor.matmul(
                out=sp[:, 0:width], lhsT=identb[:, r : r + 1].to_broadcast([P, P]), rhs=brow[:, 0:width], start=True, stop=True
            )
            return sp

        sp = spread(8, 2 * D)
        nc.scalar.copy(out=gsb[:].rearrange("p s j -> p (s j)"), in_=sp[:, 0 : 2 * D])
        for r in range(8):
            sp = spread(r, BROW)
            nc.scalar.copy(out=bias[:, BROW * r : BROW * (r + 1)], in_=sp[:, 0:BROW])

        pe4 = pe_sb[:].rearrange("p t (i f) -> p t i f", f=4)
        for s in range(2):
            g2 = gsb[:, s, :].rearrange("p (i r) -> p i r", r=2)
            nc.vector.tensor_tensor(
                out=tabs[:, 0, s, :, :].rearrange("p t (i r) -> p t i r", r=2),
                in0=pe4[:, :, :, 0:4:3],
                in1=g2.unsqueeze(1).to_broadcast([P, 2, D // 2, 2]),
                op=ALU.mult,
            )
            for r in range(2):
                nc.vector.tensor_tensor(
                    out=tabs[:, 1, s, :, :].rearrange("p t (i r) -> p t i r", r=2)[:, :, :, r],
                    in0=pe4[:, :, :, 1 + r],
                    in1=g2[:, :, 1 - r].unsqueeze(1).to_broadcast([P, 2, D // 2]),
                    op=ALU.mult,
                )
        nc.tensor.matmul(
            out=tab_ps[:].rearrange("p k s t j -> p (k s t j)"),
            lhsT=ident[:],
            rhs=tabs[:].rearrange("p k s t j -> p (k s t j)"),
            start=True,
            stop=True,
        )

        tiles = []
        vts = [(j, u) for j in range(QK_BLOCKS, NBLK) for u in range(4)]
        for n in range(2 * QK_BLOCKS):
            tiles.append((n // 2, n % 2, n, 0))
            tiles.append((n // 2, n % 2 + 2, n, 1))
            tiles.append(vts[n] + (-1, 0))
        ntile = len(tiles)
        last_unit = 2 * QK_BLOCKS - 1
        acc = {}
        ys = {}
        sss = {}
        t1s = {}
        t2s = {}
        rrs = {}
        rss = {}

        def group_of(j):
            for gi, (b0, b1) in enumerate(CODE_GROUPS):
                if b0 <= j < b1:
                    return gi, j - b0
            return None

        def mm(i):
            j, u, n, c = tiles[i]
            gi, jj = group_of(j)
            a = pacc.tile([P, NB], F32, name="acc", tag="acc")
            for g in range(PASSES):
                nc.tensor.matmul_mx(
                    out=a[:],
                    lhsT=xc[:, g, 2 * P * u : 2 * P * (u + 1)].bitcast(FP4X4),
                    lhsT_scale=xs[:, g, P * u : P * (u + 1)],
                    rhs=wc[gi][:, g, 2 * NB * jj : 2 * NB * (jj + 1)].bitcast(FP4X4),
                    rhs_scale=ws[gi][:, g, NB * jj : NB * (jj + 1)],
                    start=(g == 0),
                    stop=(g == PASSES - 1),
                )
            acc[i] = a

        def store(j, u, src):
            h0 = HB * (j % 2)
            l0 = P * (u % 2)
            nc.sync.dma_start(
                out=outs[j // 2][u // 2, h0 : h0 + HB, l0 : l0 + P, :].rearrange("h l d -> l h d"),
                in_=src.rearrange("p (h d) -> p h d", d=D),
            )

        def bias_add(i):
            j, u, n, c = tiles[i]
            bj = bias[:, NB * j : NB * (j + 1)]
            if n < 0:
                res = work.tile([P, NB], F32, name="res", tag="res", bufs=6, offset=OFF_RES, align_bytes=256)
                nc.vector.tensor_tensor(out=res[:], in0=bj, in1=acc[i][:], op=ALU.add)
                store(j, u, res[:])
                return
            if c == 0:
                y_t = work.tile([P, 2 * NB], F32, name="y", tag="y", bufs=3, offset=OFF_Y)
                ys[n] = y_t
            nc.vector.tensor_tensor(out=ys[n][:, NB * c : NB * (c + 1)], in0=bj, in1=acc[i][:], op=ALU.add)

        def squares(i):
            j, u, n, c = tiles[i]
            if c == 0:
                ss_t = work.tile([P, UH], F32, name="ss", tag="ss", bufs=2, offset=OFF_SS)
                sss[n] = ss_t
            junk = work.tile([P, NB], F32, name="junk", tag="junk", bufs=2, offset=OFF_JUNK)
            for h in range(HB):
                nc.scalar.activation(
                    out=junk[:, D * h : D * (h + 1)],
                    in_=ys[n][:, NB * c + D * h : NB * c + D * (h + 1)],
                    func=ACT.Square,
                    accum_out=sss[n][:, HB * c + h : HB * c + h + 1],
                )
            if c == 1:
                rs = work.tile([P, UH], F32, name="rs", tag="rs", bufs=3, offset=OFF_RS)
                nc.scalar.activation(out=rs[:], in_=sss[n][:], func=ACT.Abs_reciprocal_sqrt, scale=1.0 / D, bias=EPS)
                rss[n] = rs

        def gpsimd_heads(n):
            if n == 0:
                return UH
            if n == last_unit:
                return 0
            return GH

        def rope(n, lo, hi):
            s = n // 4
            t = n % 2
            gh = gpsimd_heads(n)
            nh = (hi - lo) // D
            if lo == 0:
                t1_t = work.tile([P, 2 * NB], F32, name="t1", tag="t1", bufs=2, offset=OFF_T1)
                t2_t = work.tile([P, 2 * NB], F32, name="t2", tag="t2", bufs=2, offset=OFF_T2)
                t1s[n] = t1_t
                t2s[n] = t2_t
            t1 = t1s[n]
            t2 = t2s[n]
            y = ys[n]
            mid = lo + D * gh
            if gh > 0:
                nc.gpsimd.tensor_tensor(
                    out=t1[:, lo:mid].rearrange("p (h d) -> p h d", d=D),
                    in0=y[:, lo:mid].rearrange("p (h d) -> p h d", d=D),
                    in1=tabs[:, 0, s, t, :].unsqueeze(1).to_broadcast([P, gh, D]),
                    op=ALU.mult,
                )
            nc.vector.tensor_tensor(
                out=t2[:, lo:hi].rearrange("p (h i e) -> p h i e", h=nh, e=2),
                in0=y[:, lo:hi].rearrange("p (h i e) -> p h i e", h=nh, e=2)[:, :, :, ::-1],
                in1=tab_ps[:, 1, s, t, :].rearrange("p (i e) -> p i e", e=2).unsqueeze(1).to_broadcast([P, nh, D // 2, 2]),
                op=ALU.mult,
            )
            if gh < nh:
                nc.vector.tensor_tensor(
                    out=t1[:, mid:hi].rearrange("p (h d) -> p h d", d=D),
                    in0=y[:, mid:hi].rearrange("p (h d) -> p h d", d=D),
                    in1=tab_ps[:, 0, s, t, :].unsqueeze(1).to_broadcast([P, nh - gh, D]),
                    op=ALU.mult,
                )

        def add(n, lo, hi):
            if lo == 0:
                rr_t = work.tile([P, 2 * NB], F32, name="rr", tag="rr", bufs=3, offset=OFF_RR)
                rrs[n] = rr_t
            nc.gpsimd.tensor_tensor(out=rrs[n][:, lo:hi], in0=t1s[n][:, lo:hi], in1=t2s[n][:, lo:hi], op=ALU.add)

        def scale(n):
            for c in range(2):
                res = work.tile([P, NB], F32, name="res", tag="res", bufs=6, offset=OFF_RES, align_bytes=256)
                for h in range(HB):
                    nc.scalar.activation(
                        out=res[:, D * h : D * (h + 1)],
                        in_=rrs[n][:, NB * c + D * h : NB * c + D * (h + 1)],
                        func=ACT.Copy,
                        scale=rss[n][:, HB * c + h : HB * c + h + 1],
                    )
                store(n // 2, n % 2 + 2 * c, res[:])

        for i in range(AHEAD):
            mm(i)
        for i in range(ntile):
            bias_add(i)
            if i + AHEAD < ntile:
                mm(i + AHEAD)
            if tiles[i][2] >= 0:
                squares(i)
            if i >= 1 and tiles[i - 1][2] >= 0:
                n, c = tiles[i - 1][2:4]
                if n == last_unit:
                    rope(n, NB * c, NB * (c + 1))
                    add(n, NB * c, NB * (c + 1))
                    if c == 1:
                        scale(n - 1)
                elif c == 1:
                    rope(n, 0, 2 * NB)
                    add(n, 0, 2 * NB)
                    if n >= 1:
                        scale(n - 1)
        scale(last_unit)
